import numpy as np
import ml_dtypes


def mxq(x, axis, fmt="e4m3"):
    dtype, down = {"e4m3": (ml_dtypes.float8_e4m3fn, 7), "e5m2": (ml_dtypes.float8_e5m2, 14)}[fmt]
    v = np.moveaxis(np.asarray(x, np.float32).astype(ml_dtypes.bfloat16).astype(np.float64), axis, -1)
    blocks = v.reshape(v.shape[:-1] + (-1, 32))
    amax = np.abs(blocks).max(-1, keepdims=True)
    byte = np.maximum(np.where(amax > 0, np.frexp(amax)[1] - 1 + 127, 0) - down, 1)
    scale = np.exp2(byte - 127.0)
    codes = (blocks / scale).astype(np.float32).astype(dtype).astype(np.float64)
    return np.moveaxis((codes * scale).reshape(v.shape), -1, axis)


WIDE = False


def mx_kscale(k):
    if not WIDE:
        return np.ones(k)
    levels = np.array([10, -10, 5, -5, 0])
    a = np.random.permutation(np.resize(levels, k // 512 * 4)).reshape(k // 512, 4)
    idx = np.arange(k)
    return np.exp2(a[idx // 512, idx % 128 // 32])


BF16 = ml_dtypes.bfloat16


def bf(x):
    return np.asarray(x, np.float32).astype(BF16)


def f64(x):
    return np.asarray(x).astype(np.float64)


B, S, D, DI = 4, 2048, 512, 512
EPS = 1e-12


def l2norm(v):
    n = np.sqrt(np.sum(v * v, axis=-1, keepdims=True))
    return v / np.maximum(n, EPS)


def setup_inputs():
    s = mx_kscale(D)
    return {"x": bf(np.random.standard_normal((B, S, D)) * s),
            "wk": bf(np.random.standard_normal((D, DI)) / np.sqrt(D) / s[:, None]),
            "wv": bf(np.random.standard_normal((D, DI)) / np.sqrt(D) / s[:, None])}


def reference(x, wk, wv):
    xq = mxq(f64(x), 2, "e4m3")
    k = l2norm(xq @ mxq(f64(wk), 0, "e4m3"))
    v = xq @ mxq(f64(wv), 0, "e4m3")
    return np.sum(k * v, axis=-2, keepdims=True)

@@ -1,0 +1,244 @@
+from contextlib import ExitStack
+
+import concourse.mybir as mybir
+from concourse.masks import make_identity
+
+F32 = mybir.dt.float32
+BF16 = mybir.dt.bfloat16
+U32 = mybir.dt.uint32
+U8 = mybir.dt.uint8
+FP8X4 = mybir.dt.float8_e4m3fn_x4
+ACT = mybir.ActivationFunctionType
+ALU = mybir.AluOpType
+
+P = 128
+PACK = 4
+BATCH, TOKENS, D, DI = 4, 2048, 512, 512
+EPS = 1e-12
+WORDS = D // 2
+HALVES = WORDS // P
+PAIR = 2
+CHUNK_TILES = 4
+CHUNKS_PER_BATCH = TOKENS // (CHUNK_TILES * P)
+PAIRS_PER_CHUNK = CHUNK_TILES // PAIR
+PAIRS_PER_BATCH = CHUNKS_PER_BATCH * PAIRS_PER_CHUNK
+N_PAIRS = BATCH * PAIRS_PER_BATCH
+FILL = 3
+SUM_PARTS = 2 * PAIR
+
+FLOPS = 2 * 2 * BATCH * TOKENS * D * DI
+
+
+def tile_hydraencoderlayer_pa_t_kernel(tc, x, wk, wv, out):
+    nc = tc.nc
+    with ExitStack() as ctx:
+        ctx.enter_context(tc.manual_schedule())
+        consts = ctx.enter_context(tc.tile_pool(name="consts", bufs=1))
+        x_pool = ctx.enter_context(tc.tile_pool(name="x_pool", bufs=BATCH * CHUNKS_PER_BATCH))
+        stage = ctx.enter_context(tc.tile_pool(name="stage", bufs=2))
+        operands = ctx.enter_context(tc.tile_pool(name="operands", bufs=3))
+        work = ctx.enter_context(tc.tile_pool(name="work", bufs=4))
+        sums = ctx.enter_context(tc.tile_pool(name="sums", bufs=2))
+        psum_t = ctx.enter_context(tc.psum_pool(name="psum_t", bufs=1))
+        psum_a = ctx.enter_context(tc.psum_pool(name="psum_a", bufs=3))
+        psum_v = ctx.enter_context(tc.psum_pool(name="psum_v", bufs=3))
+        psum_s = ctx.enter_context(tc.psum_pool(name="psum_s", bufs=1))
+
+        w_raw = {}
+        for label, w in (("wk", wk), ("wv", wv)):
+            w_raw[label] = consts.tile([P, PACK, DI], BF16, name="%s_raw" % label)
+            nc.sync.dma_start(
+                out=w_raw[label][:].rearrange("q (u e) c -> q u (e c)", u=HALVES),
+                in_=w.rearrange("(u q e) c -> q u (e c)", u=HALVES, e=2),
+            )
+        x_chunks = []
+        for b in range(BATCH):
+            chunks = x[b].rearrange("(p c t) k -> c p (t k)", c=CHUNKS_PER_BATCH, t=CHUNK_TILES)
+            for c in range(CHUNKS_PER_BATCH):
+                x_sb = x_pool.tile([P, CHUNK_TILES * D], BF16)
+                nc.sync.dma_start(out=x_sb[:], in_=chunks[c])
+                x_chunks.append(x_sb)
+
+        ident = consts.tile([P, P], F32)
+        make_identity(nc, ident[:])
+        ones = consts.tile([P, P], F32)
+        nc.vector.memset(ones[:], 1.0)
+        warm = consts.tile([P, 1], F32)
+        nc.scalar.activation(out=warm[:], in_=ones[:, 0:1], func=ACT.Sqrt)
+
+        w_grouped = {}
+        w_codes = {}
+        w_scales = {}
+        for label in ("wk", "wv"):
+            w_grouped[label] = consts.tile(
+                [P, DI, PACK], BF16, name="%s_grouped" % label, align_bytes=64
+            )
+            w_codes[label] = consts.tile([P, DI], U32, name="%s_codes" % label, align_bytes=64)
+            w_scales[label] = consts.tile([P, DI], U8, name="%s_scales" % label, align_bytes=64)
+
+        def quantise_weight(label):
+            nc.vector.quantize_mx(
+                out=w_codes[label][:].bitcast(FP8X4),
+                scales=w_scales[label][:],
+                in_=w_grouped[label][:].rearrange("q c t -> q (c t)"),
+            )
+
+        nc.vector.tensor_copy(out=w_grouped["wk"][:], in_=w_raw["wk"][:].rearrange("q t c -> q c t"))
+        nc.scalar.copy(out=w_grouped["wv"][:], in_=w_raw["wv"][:].rearrange("q t c -> q c t"))
+        quantise_weight("wk")
+
+        xt, grouped, x_codes, x_scales = {}, {}, {}, {}
+        a_ps, v_ps, a_sb = {}, {}, {}
+        norm2, excess, norm, rnorm = {}, {}, {}, {}
+        prod, acc, total = {}, {}, {}
+
+        def transpose_x(n):
+            x_words = x_chunks[n // PAIRS_PER_CHUNK][:].bitcast(F32)
+            first_tile = (n % PAIRS_PER_CHUNK) * PAIR
+            xt[n] = psum_t.tile([P, PAIR, HALVES, P], F32, name="xt")
+            for j in range(PAIR):
+                for u in range(HALVES):
+                    w0 = (first_tile + j) * WORDS + u * P
+                    nc.tensor.transpose(xt[n][:, j, u, :], x_words[:, w0 : w0 + P], ident[:])
+
+        def regroup_x(n):
+            grouped[n] = stage.tile([P, PAIR * P * PACK], BF16, name="grouped", align_bytes=64)
+            nc.vector.tensor_copy(
+                out=grouped[n][:].bitcast(F32).rearrange("p (j r u) -> p j r u", j=PAIR, u=HALVES),
+                in_=xt[n][:].rearrange("p j u r -> p j r u"),
+            )
+
+        def quantise_x(n):
+            x_codes[n] = operands.tile([P, PAIR * P], U32, name="x_codes", align_bytes=64)
+            x_scales[n] = operands.tile([P, PAIR * P], U8, name="x_scales", align_bytes=64)
+            nc.vector.quantize_mx(
+                out=x_codes[n][:].bitcast(FP8X4), scales=x_scales[n][:], in_=grouped[n][:]
+            )
+
+        def mx_pass(bank, n, j, label):
+            cols = slice(j * P, (j + 1) * P)
+            nc.tensor.matmul_mx(
+                out=bank[:],
+                lhsT=x_codes[n][:, cols].bitcast(FP8X4),
+                lhsT_scale=x_scales[n][:, cols],
+                rhs=w_codes[label][:].bitcast(FP8X4),
+                rhs_scale=w_scales[label][:],
+                start=True,
+                stop=True,
+            )
+
+        def pass_a(n, j):
+            a_ps[n, j] = psum_a.tile([P, DI], F32, name="a_ps")
+            mx_pass(a_ps[n, j], n, j, "wk")
+
+        def pass_v(n, j):
+            v_ps[n, j] = psum_v.tile([P, DI], F32, name="v_ps")
+            mx_pass(v_ps[n, j], n, j, "wv")
+
+        def square_sum(n, j):
+            if j == 0:
+                norm2[n] = work.tile([P, PAIR], F32, name="norm2")
+            squares = work.tile([P, DI], BF16, name="squares")
+            nc.scalar.activation(
+                out=squares[:], in_=a_ps[n, j][:], func=ACT.Square,
+                accum_out=norm2[n][:, j : j + 1],
+            )
+
+        def copy_a(n, j):
+            a_sb[n, j] = work.tile([P, DI], F32, name="a_sb")
+            nc.scalar.copy(out=a_sb[n, j][:], in_=a_ps[n, j][:])
+
+        def clamp_norm2(n):
+            excess[n] = work.tile([P, PAIR], F32, name="excess")
+            nc.scalar.activation(out=excess[n][:], in_=norm2[n][:], func=ACT.Relu, bias=-EPS * EPS)
+
+        def root_norm(n):
+            norm[n] = work.tile([P, PAIR], F32, name="norm")
+            nc.scalar.activation(out=norm[n][:], in_=excess[n][:], func=ACT.Sqrt, bias=EPS * EPS)
+
+        def invert_norm(n):
+            rnorm[n] = work.tile([P, PAIR], F32, name="rnorm")
+            nc.vector.reciprocal(out=rnorm[n][:], in_=norm[n][:])
+
+        def product(n, j):
+            if j == 0:
+                prod[n] = work.tile([P, PAIR, DI], F32, name="prod")
+            nc.vector.scalar_tensor_tensor(
+                out=prod[n][:, j, :],
+                in0=a_sb[n, j][:],
+                scalar=rnorm[n][:, j : j + 1],
+                in1=v_ps[n, j][:],
+                op0=ALU.mult,
+                op1=ALU.mult,
+            )
+
+        def accumulate(n):
+            b, q = divmod(n, PAIRS_PER_BATCH)
+            if q == 1:
+                acc[b] = sums.tile([P, PAIR, DI], F32, name="acc")
+                nc.gpsimd.tensor_tensor(out=acc[b][:], in0=prod[n - 1][:], in1=prod[n][:], op=ALU.add)
+            elif 1 < q < PAIRS_PER_BATCH - 1:
+                nc.gpsimd.tensor_tensor(out=acc[b][:], in0=acc[b][:], in1=prod[n][:], op=ALU.add)
+
+        def sum_partitions(b, i):
+            last = prod[(b + 1) * PAIRS_PER_BATCH - 1]
+            parts = [last[:, 0, :], last[:, 1, :], acc[b][:, 0, :], acc[b][:, 1, :]]
+            if i == 0:
+                total[b] = psum_s.tile([P, DI], F32, name="total")
+            nc.tensor.matmul(
+                out=total[b][:], lhsT=ones[:], rhs=parts[i],
+                start=(i == 0), stop=(i == SUM_PARTS - 1),
+            )
+
+        def store(b):
+            result = sums.tile([P, DI], F32, name="result")
+            nc.vector.tensor_copy(out=result[:], in_=total[b][:])
+            nc.sync.dma_start(out=out[b], in_=result[0:1, :])
+
+        def live(n):
+            return 0 <= n < N_PAIRS
+
+        def step(n):
+            if live(n + 1):
+                pass_a(n + 1, 0)
+            if live(n):
+                pass_v(n, 0)
+            if live(n + 3):
+                transpose_x(n + 3)
+            if live(n):
+                square_sum(n, 0)
+            if live(n - 1):
+                root_norm(n - 1)
+            if live(n):
+                copy_a(n, 0)
+                square_sum(n, 1)
+                copy_a(n, 1)
+                clamp_norm2(n)
+            if live(n + 1):
+                pass_a(n + 1, 1)
+            if live(n - 1):
+                invert_norm(n - 1)
+            if live(n + 2):
+                quantise_x(n + 2)
+            if live(n - 1):
+                product(n - 1, 0)
+                product(n - 1, 1)
+            if live(n):
+                pass_v(n, 1)
+            if live(n - 1):
+                accumulate(n - 1)
+            since_last = n - PAIRS_PER_BATCH
+            if since_last >= 0:
+                b, i = divmod(since_last, PAIRS_PER_BATCH)
+                if i < SUM_PARTS:
+                    sum_partitions(b, i)
+                elif i == SUM_PARTS:
+                    store(b)
+            if live(n + 3):
+                regroup_x(n + 3)
+
+        for n in range(-FILL, -1):
+            step(n)
+        quantise_weight("wv")
+        for n in range(-1, N_PAIRS + SUM_PARTS + 1):
+            step(n)

@@ -176,9 +176,9 @@ def tile_hydraencoderlayer_pa_t_kernel(tc, x, wk, wv, out):
             b, q = divmod(n, PAIRS_PER_BATCH)
             if q == 1:
                 acc[b] = sums.tile([P, PAIR, DI], F32, name="acc")
-                nc.gpsimd.tensor_tensor(out=acc[b][:], in0=prod[n - 1][:], in1=prod[n][:], op=ALU.add)
+                nc.vector.tensor_tensor(out=acc[b][:], in0=prod[n - 1][:], in1=prod[n][:], op=ALU.add)
             elif 1 < q < PAIRS_PER_BATCH - 1:
-                nc.gpsimd.tensor_tensor(out=acc[b][:], in0=acc[b][:], in1=prod[n][:], op=ALU.add)
+                nc.vector.tensor_tensor(out=acc[b][:], in0=acc[b][:], in1=prod[n][:], op=ALU.add)
 
         def sum_partitions(b, i):
             last = prod[(b + 1) * PAIRS_PER_BATCH - 1]

@@ -24,7 +24,7 @@ PAIRS_PER_CHUNK = CHUNK_TILES // PAIR
 PAIRS_PER_BATCH = CHUNKS_PER_BATCH * PAIRS_PER_CHUNK
 N_PAIRS = BATCH * PAIRS_PER_BATCH
 FILL = 3
-SUM_PARTS = 2 * PAIR
+E_BLOCKS = DI // P
 
 FLOPS = 2 * 2 * BATCH * TOKENS * D * DI
 
@@ -38,7 +38,6 @@ def tile_hydraencoderlayer_pa_t_kernel(tc, x, wk, wv, out):
         stage = ctx.enter_context(tc.tile_pool(name="stage", bufs=2))
         operands = ctx.enter_context(tc.tile_pool(name="operands", bufs=3))
         work = ctx.enter_context(tc.tile_pool(name="work", bufs=4))
-        sums = ctx.enter_context(tc.tile_pool(name="sums", bufs=2))
         psum_t = ctx.enter_context(tc.psum_pool(name="psum_t", bufs=1))
         psum_a = ctx.enter_context(tc.psum_pool(name="psum_a", bufs=3))
         psum_v = ctx.enter_context(tc.psum_pool(name="psum_v", bufs=3))
@@ -61,10 +60,12 @@ def tile_hydraencoderlayer_pa_t_kernel(tc, x, wk, wv, out):
 
         ident = consts.tile([P, P], F32)
         make_identity(nc, ident[:])
-        ones = consts.tile([P, P], F32)
-        nc.vector.memset(ones[:], 1.0)
+        out_cols = consts.tile([P, P], F32)
+        nc.vector.memset(out_cols[:], 0.0)
+        one = consts.tile([P, 1], F32)
+        nc.vector.memset(one[:], 1.0)
         warm = consts.tile([P, 1], F32)
-        nc.scalar.activation(out=warm[:], in_=ones[:, 0:1], func=ACT.Sqrt)
+        nc.scalar.activation(out=warm[:], in_=one[:], func=ACT.Sqrt)
 
         w_grouped = {}
         w_codes = {}
@@ -90,7 +91,7 @@ def tile_hydraencoderlayer_pa_t_kernel(tc, x, wk, wv, out):
         xt, grouped, x_codes, x_scales = {}, {}, {}, {}
         a_ps, v_ps, a_sb = {}, {}, {}
         norm2, excess, norm, rnorm = {}, {}, {}, {}
-        prod, acc, total = {}, {}, {}
+        prod, token_sums = {}, {}
 
         def transpose_x(n):
             x_words = x_chunks[n // PAIRS_PER_CHUNK][:].bitcast(F32)
@@ -172,28 +173,28 @@ def tile_hydraencoderlayer_pa_t_kernel(tc, x, wk, wv, out):
                 op1=ALU.mult,
             )
 
-        def accumulate(n):
+        def add_tokens(n):
             b, q = divmod(n, PAIRS_PER_BATCH)
-            if q == 1:
-                acc[b] = sums.tile([P, PAIR, DI], F32, name="acc")
-                nc.vector.tensor_tensor(out=acc[b][:], in0=prod[n - 1][:], in1=prod[n][:], op=ALU.add)
-            elif 1 < q < PAIRS_PER_BATCH - 1:
-                nc.vector.tensor_tensor(out=acc[b][:], in0=acc[b][:], in1=prod[n][:], op=ALU.add)
+            if q == 0:
+                token_sums[b] = psum_s.tile([P, E_BLOCKS, P], F32, name="token_sums")
+            for j in range(PAIR):
+                for i in range(E_BLOCKS):
+                    nc.tensor.matmul(
+                        out=token_sums[b][:, i, :],
+                        lhsT=prod[n][:, j, i * P : (i + 1) * P],
+                        rhs=ident[:],
+                        is_transpose=True,
+                        start=(q == 0 and j == 0 and i == 0),
+                        stop=(q == PAIRS_PER_BATCH - 1 and j == PAIR - 1 and i == E_BLOCKS - 1),
+                    )
 
-        def sum_partitions(b, i):
-            last = prod[(b + 1) * PAIRS_PER_BATCH - 1]
-            parts = [last[:, 0, :], last[:, 1, :], acc[b][:, 0, :], acc[b][:, 1, :]]
-            if i == 0:
-                total[b] = psum_s.tile([P, DI], F32, name="total")
-            nc.tensor.matmul(
-                out=total[b][:], lhsT=ones[:], rhs=parts[i],
-                start=(i == 0), stop=(i == SUM_PARTS - 1),
+        def add_partitions(b):
+            nc.vector.tensor_reduce(
+                out=out_cols[:, b * E_BLOCKS : (b + 1) * E_BLOCKS],
+                in_=token_sums[b][:],
+                axis=mybir.AxisListType.X,
+                op=ALU.add,
             )
-
-        def store(b):
-            result = sums.tile([P, DI], F32, name="result")
-            nc.vector.tensor_copy(out=result[:], in_=total[b][:])
-            nc.sync.dma_start(out=out[b], in_=result[0:1, :])
 
         def live(n):
             return 0 <= n < N_PAIRS
@@ -205,6 +206,8 @@ def tile_hydraencoderlayer_pa_t_kernel(tc, x, wk, wv, out):
                 pass_v(n, 0)
             if live(n + 3):
                 transpose_x(n + 3)
+            if live(n - 2):
+                add_tokens(n - 2)
             if live(n):
                 square_sum(n, 0)
             if live(n - 1):
@@ -225,20 +228,22 @@ def tile_hydraencoderlayer_pa_t_kernel(tc, x, wk, wv, out):
                 product(n - 1, 1)
             if live(n):
                 pass_v(n, 1)
-            if live(n - 1):
-                accumulate(n - 1)
-            since_last = n - PAIRS_PER_BATCH
-            if since_last >= 0:
-                b, i = divmod(since_last, PAIRS_PER_BATCH)
-                if i < SUM_PARTS:
-                    sum_partitions(b, i)
-                elif i == SUM_PARTS:
-                    store(b)
+            if live(n - 2) and (n - 2) % PAIRS_PER_BATCH == PAIRS_PER_BATCH - 1:
+                add_partitions((n - 2) // PAIRS_PER_BATCH)
             if live(n + 3):
                 regroup_x(n + 3)
 
         for n in range(-FILL, -1):
             step(n)
         quantise_weight("wv")
-        for n in range(-1, N_PAIRS + SUM_PARTS + 1):
+        for n in range(-1, N_PAIRS + 2):
             step(n)
+
+        out_rows_ps = psum_t.tile([P, P], F32, name="xt")
+        nc.tensor.transpose(out_rows_ps[:], out_cols[:], ident[:])
+        out_rows = consts.tile([P, P], F32)
+        nc.vector.tensor_copy(out=out_rows[:], in_=out_rows_ps[:])
+        nc.sync.dma_start(
+            out=out.rearrange("b o (i e) -> (b o i) e", i=E_BLOCKS),
+            in_=out_rows[0 : BATCH * E_BLOCKS, :],
+        )

@@ -62,10 +62,8 @@ def tile_hydraencoderlayer_pa_t_kernel(tc, x, wk, wv, out):
         make_identity(nc, ident[:])
         out_cols = consts.tile([P, P], F32)
         nc.vector.memset(out_cols[:], 0.0)
-        one = consts.tile([P, 1], F32)
-        nc.vector.memset(one[:], 1.0)
-        warm = consts.tile([P, 1], F32)
-        nc.scalar.activation(out=warm[:], in_=one[:], func=ACT.Sqrt)
+        minus_half = consts.tile([P, PAIR], F32)
+        nc.vector.memset(minus_half[:], -0.5)
 
         w_grouped = {}
         w_codes = {}
@@ -90,7 +88,7 @@ def tile_hydraencoderlayer_pa_t_kernel(tc, x, wk, wv, out):
 
         xt, grouped, x_codes, x_scales = {}, {}, {}, {}
         a_ps, v_ps, a_sb = {}, {}, {}
-        norm2, excess, norm, rnorm = {}, {}, {}, {}
+        norm2, rnorm = {}, {}
         prod, token_sums = {}, {}
 
         def transpose_x(n):
@@ -149,17 +147,11 @@ def tile_hydraencoderlayer_pa_t_kernel(tc, x, wk, wv, out):
             a_sb[n, j] = work.tile([P, DI], F32, name="a_sb")
             nc.scalar.copy(out=a_sb[n, j][:], in_=a_ps[n, j][:])
 
-        def clamp_norm2(n):
-            excess[n] = work.tile([P, PAIR], F32, name="excess")
-            nc.scalar.activation(out=excess[n][:], in_=norm2[n][:], func=ACT.Relu, bias=-EPS * EPS)
-
-        def root_norm(n):
-            norm[n] = work.tile([P, PAIR], F32, name="norm")
-            nc.scalar.activation(out=norm[n][:], in_=excess[n][:], func=ACT.Sqrt, bias=EPS * EPS)
-
         def invert_norm(n):
+            clamped = work.tile([P, PAIR], F32, name="clamped")
+            nc.gpsimd.tensor_scalar_max(out=clamped[:], in0=norm2[n][:], scalar1=EPS * EPS)
             rnorm[n] = work.tile([P, PAIR], F32, name="rnorm")
-            nc.vector.reciprocal(out=rnorm[n][:], in_=norm[n][:])
+            nc.gpsimd.tensor_tensor(out=rnorm[n][:], in0=clamped[:], in1=minus_half[:], op=ALU.pow)
 
         def product(n, j):
             if j == 0:
@@ -210,17 +202,12 @@ def tile_hydraencoderlayer_pa_t_kernel(tc, x, wk, wv, out):
                 add_tokens(n - 2)
             if live(n):
                 square_sum(n, 0)
-            if live(n - 1):
-                root_norm(n - 1)
-            if live(n):
                 copy_a(n, 0)
                 square_sum(n, 1)
                 copy_a(n, 1)
-                clamp_norm2(n)
+                invert_norm(n)
             if live(n + 1):
                 pass_a(n + 1, 1)
-            if live(n - 1):
-                invert_norm(n - 1)
             if live(n + 2):
                 quantise_x(n + 2)
             if live(n - 1):

@@ -208,10 +208,11 @@ def tile_hydraencoderlayer_pa_t_kernel(tc, x, wk, wv, out):
                 invert_norm(n)
             if live(n + 1):
                 pass_a(n + 1, 1)
+            if live(n - 1):
+                product(n - 1, 0)
             if live(n + 2):
                 quantise_x(n + 2)
             if live(n - 1):
-                product(n - 1, 0)
                 product(n - 1, 1)
             if live(n):
                 pass_v(n, 1)

@@ -23,7 +23,7 @@ CHUNKS_PER_BATCH = TOKENS // (CHUNK_TILES * P)
 PAIRS_PER_CHUNK = CHUNK_TILES // PAIR
 PAIRS_PER_BATCH = CHUNKS_PER_BATCH * PAIRS_PER_CHUNK
 N_PAIRS = BATCH * PAIRS_PER_BATCH
-FILL = 3
+W_SPLIT = 320
 E_BLOCKS = DI // P
 
 FLOPS = 2 * 2 * BATCH * TOKENS * D * DI
@@ -36,27 +36,35 @@ def tile_hydraencoderlayer_pa_t_kernel(tc, x, wk, wv, out):
         consts = ctx.enter_context(tc.tile_pool(name="consts", bufs=1))
         x_pool = ctx.enter_context(tc.tile_pool(name="x_pool", bufs=BATCH * CHUNKS_PER_BATCH))
         stage = ctx.enter_context(tc.tile_pool(name="stage", bufs=2))
-        operands = ctx.enter_context(tc.tile_pool(name="operands", bufs=3))
-        work = ctx.enter_context(tc.tile_pool(name="work", bufs=4))
+        operands = ctx.enter_context(tc.tile_pool(name="operands", bufs=4))
+        work = ctx.enter_context(tc.tile_pool(name="work", bufs=6))
         psum_t = ctx.enter_context(tc.psum_pool(name="psum_t", bufs=1))
         psum_a = ctx.enter_context(tc.psum_pool(name="psum_a", bufs=3))
         psum_v = ctx.enter_context(tc.psum_pool(name="psum_v", bufs=3))
         psum_s = ctx.enter_context(tc.psum_pool(name="psum_s", bufs=1))
 
         w_raw = {}
-        for label, w in (("wk", wk), ("wv", wv)):
+
+        def load_weight(label, w):
             w_raw[label] = consts.tile([P, PACK, DI], BF16, name="%s_raw" % label)
             nc.sync.dma_start(
                 out=w_raw[label][:].rearrange("q (u e) c -> q u (e c)", u=HALVES),
                 in_=w.rearrange("(u q e) c -> q u (e c)", u=HALVES, e=2),
             )
+        load_weight("wk", wk)
         x_chunks = []
         for b in range(BATCH):
             chunks = x[b].rearrange("(p c t) k -> c p (t k)", c=CHUNKS_PER_BATCH, t=CHUNK_TILES)
             for c in range(CHUNKS_PER_BATCH):
                 x_sb = x_pool.tile([P, CHUNK_TILES * D], BF16)
-                nc.sync.dma_start(out=x_sb[:], in_=chunks[c])
                 x_chunks.append(x_sb)
+                if b == 0 and c == 0:
+                    pair_cols = PAIR * D
+                    nc.sync.dma_start(out=x_sb[:, :pair_cols], in_=chunks[c][:, :pair_cols])
+                    load_weight("wv", wv)
+                    nc.sync.dma_start(out=x_sb[:, pair_cols:], in_=chunks[c][:, pair_cols:])
+                else:
+                    nc.sync.dma_start(out=x_sb[:], in_=chunks[c])
 
         ident = consts.tile([P, P], F32)
         make_identity(nc, ident[:])
@@ -82,37 +90,57 @@ def tile_hydraencoderlayer_pa_t_kernel(tc, x, wk, wv, out):
                 in_=w_grouped[label][:].rearrange("q c t -> q (c t)"),
             )
 
-        nc.vector.tensor_copy(out=w_grouped["wk"][:], in_=w_raw["wk"][:].rearrange("q t c -> q c t"))
-        nc.scalar.copy(out=w_grouped["wv"][:], in_=w_raw["wv"][:].rearrange("q t c -> q c t"))
-        quantise_weight("wk")
+        def interleave_weight(label):
+            by_column = w_raw[label][:].rearrange("q t c -> q c t")
+            grouped_w = w_grouped[label]
+            nc.vector.tensor_copy(out=grouped_w[:, :W_SPLIT, :], in_=by_column[:, :W_SPLIT, :])
+            nc.scalar.copy(out=grouped_w[:, W_SPLIT:, :], in_=by_column[:, W_SPLIT:, :])
 
         xt, grouped, x_codes, x_scales = {}, {}, {}, {}
         a_ps, v_ps, a_sb = {}, {}, {}
         norm2, rnorm = {}, {}
-        prod, token_sums = {}, {}
+        prod, pair_sum, token_sums = {}, {}, {}
 
-        def transpose_x(n):
+        def transpose_tile(bank, n, j):
             x_words = x_chunks[n // PAIRS_PER_CHUNK][:].bitcast(F32)
-            first_tile = (n % PAIRS_PER_CHUNK) * PAIR
-            xt[n] = psum_t.tile([P, PAIR, HALVES, P], F32, name="xt")
+            first_word = ((n % PAIRS_PER_CHUNK) * PAIR + j) * WORDS
+            for u in range(HALVES):
+                w0 = first_word + u * P
+                nc.tensor.transpose(bank[:, j, u, :], x_words[:, w0 : w0 + P], ident[:])
+
+        def new_xt(pool=psum_t, name="xt"):
+            return pool.tile([P, PAIR, HALVES, P], F32, name=name)
+
+        def transpose_x(n, bank):
+            xt[n] = bank
             for j in range(PAIR):
-                for u in range(HALVES):
-                    w0 = (first_tile + j) * WORDS + u * P
-                    nc.tensor.transpose(xt[n][:, j, u, :], x_words[:, w0 : w0 + P], ident[:])
+                transpose_tile(bank, n, j)
+
+        def regroup_tiles(n, tiles, bank, copy):
+            if n not in grouped:
+                grouped[n] = stage.tile([P, PAIR * P * PACK], BF16, name="grouped", align_bytes=64)
+            words = grouped[n][:].bitcast(F32).rearrange("p (j r u) -> p j r u", j=PAIR, u=HALVES)
+            copy(
+                out=words[:, tiles, :, :],
+                in_=bank[:].rearrange("p j u r -> p j r u")[:, tiles, :, :],
+            )
 
         def regroup_x(n):
-            grouped[n] = stage.tile([P, PAIR * P * PACK], BF16, name="grouped", align_bytes=64)
-            nc.vector.tensor_copy(
-                out=grouped[n][:].bitcast(F32).rearrange("p (j r u) -> p j r u", j=PAIR, u=HALVES),
-                in_=xt[n][:].rearrange("p j u r -> p j r u"),
+            regroup_tiles(n, slice(0, PAIR), xt[n], nc.vector.tensor_copy)
+
+        def quantise_tiles(n, tiles):
+            if n not in x_codes:
+                x_codes[n] = operands.tile([P, PAIR * P], U32, name="x_codes", align_bytes=64)
+                x_scales[n] = operands.tile([P, PAIR * P], U8, name="x_scales", align_bytes=64)
+            cols = slice(tiles.start * P, tiles.stop * P)
+            nc.vector.quantize_mx(
+                out=x_codes[n][:, cols].bitcast(FP8X4),
+                scales=x_scales[n][:, cols],
+                in_=grouped[n][:, tiles.start * P * PACK : tiles.stop * P * PACK],
             )
 
         def quantise_x(n):
-            x_codes[n] = operands.tile([P, PAIR * P], U32, name="x_codes", align_bytes=64)
-            x_scales[n] = operands.tile([P, PAIR * P], U8, name="x_scales", align_bytes=64)
-            nc.vector.quantize_mx(
-                out=x_codes[n][:].bitcast(FP8X4), scales=x_scales[n][:], in_=grouped[n][:]
-            )
+            quantise_tiles(n, slice(0, PAIR))
 
         def mx_pass(bank, n, j, label):
             cols = slice(j * P, (j + 1) * P)
@@ -143,9 +171,9 @@ def tile_hydraencoderlayer_pa_t_kernel(tc, x, wk, wv, out):
                 accum_out=norm2[n][:, j : j + 1],
             )
 
-        def copy_a(n, j):
+        def copy_a(n, j, copy=nc.scalar.copy):
             a_sb[n, j] = work.tile([P, DI], F32, name="a_sb")
-            nc.scalar.copy(out=a_sb[n, j][:], in_=a_ps[n, j][:])
+            copy(out=a_sb[n, j][:], in_=a_ps[n, j][:])
 
         def invert_norm(n):
             clamped = work.tile([P, PAIR], F32, name="clamped")
@@ -165,19 +193,31 @@ def tile_hydraencoderlayer_pa_t_kernel(tc, x, wk, wv, out):
                 op1=ALU.mult,
             )
 
+        def add_pair(n):
+            if n % 4 != 1:
+                return
+            pair_sum[n] = work.tile([P, DI], F32, name="pair_sum")
+            nc.vector.tensor_tensor(
+                out=pair_sum[n][:], in0=prod[n][:, 0, :], in1=prod[n][:, 1, :], op=ALU.add
+            )
+
         def add_tokens(n):
             b, q = divmod(n, PAIRS_PER_BATCH)
             if q == 0:
                 token_sums[b] = psum_s.tile([P, E_BLOCKS, P], F32, name="token_sums")
-            for j in range(PAIR):
+            if n in pair_sum:
+                tiles = [pair_sum[n][:]]
+            else:
+                tiles = [prod[n][:, j, :] for j in range(PAIR)]
+            for k, tile in enumerate(tiles):
                 for i in range(E_BLOCKS):
                     nc.tensor.matmul(
                         out=token_sums[b][:, i, :],
-                        lhsT=prod[n][:, j, i * P : (i + 1) * P],
+                        lhsT=tile[:, i * P : (i + 1) * P],
                         rhs=ident[:],
                         is_transpose=True,
-                        start=(q == 0 and j == 0 and i == 0),
-                        stop=(q == PAIRS_PER_BATCH - 1 and j == PAIR - 1 and i == E_BLOCKS - 1),
+                        start=(q == 0 and k == 0 and i == 0),
+                        stop=(q == PAIRS_PER_BATCH - 1 and k == len(tiles) - 1 and i == E_BLOCKS - 1),
                     )
 
         def add_partitions(b):
@@ -197,14 +237,18 @@ def tile_hydraencoderlayer_pa_t_kernel(tc, x, wk, wv, out):
             if live(n):
                 pass_v(n, 0)
             if live(n + 3):
-                transpose_x(n + 3)
+                transpose_x(n + 3, new_xt())
             if live(n - 2):
                 add_tokens(n - 2)
             if live(n):
                 square_sum(n, 0)
-                copy_a(n, 0)
-                square_sum(n, 1)
-                copy_a(n, 1)
+                if n < N_PAIRS - 1:
+                    copy_a(n, 0)
+                    square_sum(n, 1)
+                    copy_a(n, 1)
+                else:
+                    square_sum(n, 1)
+                    copy_a(n, 0)
                 invert_norm(n)
             if live(n + 1):
                 pass_a(n + 1, 1)
@@ -214,17 +258,35 @@ def tile_hydraencoderlayer_pa_t_kernel(tc, x, wk, wv, out):
                 quantise_x(n + 2)
             if live(n - 1):
                 product(n - 1, 1)
+            if n == N_PAIRS - 1:
+                copy_a(n, 1, copy=nc.vector.tensor_copy)
             if live(n):
                 pass_v(n, 1)
             if live(n - 2) and (n - 2) % PAIRS_PER_BATCH == PAIRS_PER_BATCH - 1:
                 add_partitions((n - 2) // PAIRS_PER_BATCH)
             if live(n + 3):
                 regroup_x(n + 3)
+            if live(n - 1):
+                add_pair(n - 1)
 
-        for n in range(-FILL, -1):
-            step(n)
+        interleave_weight("wk")
+        quantise_weight("wk")
+        banks = [new_xt(), new_xt(psum_v, "v_ps")]
+        for j in range(PAIR):
+            transpose_tile(banks[j], 0, j)
+        for j in range(PAIR):
+            regroup_tiles(0, slice(j, j + 1), banks[j], nc.scalar.copy)
+            quantise_tiles(0, slice(j, j + 1))
+        for j in range(PAIR):
+            pass_a(0, j)
+        interleave_weight("wv")
+        transpose_x(1, new_xt(psum_v, "v_ps"))
+        regroup_x(1)
         quantise_weight("wv")
-        for n in range(-1, N_PAIRS + 2):
+        quantise_x(1)
+        transpose_x(2, new_xt())
+        regroup_x(2)
+        for n in range(N_PAIRS + 2):
             step(n)
 
         out_rows_ps = psum_t.tile([P, P], F32, name="xt")

@@ -99,7 +99,7 @@ def tile_hydraencoderlayer_pa_t_kernel(tc, x, wk, wv, out):
         xt, grouped, x_codes, x_scales = {}, {}, {}, {}
         a_ps, v_ps, a_sb = {}, {}, {}
         norm2, rnorm = {}, {}
-        prod, pair_sum, token_sums = {}, {}, {}
+        prod, token_sums = {}, {}
 
         def transpose_tile(bank, n, j):
             x_words = x_chunks[n // PAIRS_PER_CHUNK][:].bitcast(F32)
@@ -193,31 +193,19 @@ def tile_hydraencoderlayer_pa_t_kernel(tc, x, wk, wv, out):
                 op1=ALU.mult,
             )
 
-        def add_pair(n):
-            if n % 4 != 1:
-                return
-            pair_sum[n] = work.tile([P, DI], F32, name="pair_sum")
-            nc.vector.tensor_tensor(
-                out=pair_sum[n][:], in0=prod[n][:, 0, :], in1=prod[n][:, 1, :], op=ALU.add
-            )
-
         def add_tokens(n):
             b, q = divmod(n, PAIRS_PER_BATCH)
             if q == 0:
                 token_sums[b] = psum_s.tile([P, E_BLOCKS, P], F32, name="token_sums")
-            if n in pair_sum:
-                tiles = [pair_sum[n][:]]
-            else:
-                tiles = [prod[n][:, j, :] for j in range(PAIR)]
-            for k, tile in enumerate(tiles):
+            for j in range(PAIR):
                 for i in range(E_BLOCKS):
                     nc.tensor.matmul(
                         out=token_sums[b][:, i, :],
-                        lhsT=tile[:, i * P : (i + 1) * P],
+                        lhsT=prod[n][:, j, i * P : (i + 1) * P],
                         rhs=ident[:],
                         is_transpose=True,
-                        start=(q == 0 and k == 0 and i == 0),
-                        stop=(q == PAIRS_PER_BATCH - 1 and k == len(tiles) - 1 and i == E_BLOCKS - 1),
+                        start=(q == 0 and j == 0 and i == 0),
+                        stop=(q == PAIRS_PER_BATCH - 1 and j == PAIR - 1 and i == E_BLOCKS - 1),
                     )
 
         def add_partitions(b):
@@ -266,8 +254,6 @@ def tile_hydraencoderlayer_pa_t_kernel(tc, x, wk, wv, out):
                 add_partitions((n - 2) // PAIRS_PER_BATCH)
             if live(n + 3):
                 regroup_x(n + 3)
-            if live(n - 1):
-                add_pair(n - 1)
 
         interleave_weight("wk")
         quantise_weight("wk")

@@ -70,6 +70,8 @@ def tile_hydraencoderlayer_pa_t_kernel(tc, x, wk, wv, out):
         make_identity(nc, ident[:])
         out_cols = consts.tile([P, P], F32)
         nc.vector.memset(out_cols[:], 0.0)
+        zeros = consts.tile([P, DI], BF16)
+        nc.vector.memset(zeros[:], 0.0)
         minus_half = consts.tile([P, PAIR], F32)
         nc.vector.memset(minus_half[:], -0.5)
 
@@ -95,6 +97,11 @@ def tile_hydraencoderlayer_pa_t_kernel(tc, x, wk, wv, out):
             grouped_w = w_grouped[label]
             nc.vector.tensor_copy(out=grouped_w[:, :W_SPLIT, :], in_=by_column[:, :W_SPLIT, :])
             nc.scalar.copy(out=grouped_w[:, W_SPLIT:, :], in_=by_column[:, W_SPLIT:, :])
+
+        def warm_up(count):
+            bank = psum_s.tile([P, DI], F32, name="token_sums")
+            for k in range(count):
+                nc.tensor.matmul(out=bank[:], lhsT=zeros[:, :P], rhs=zeros[:], start=True, stop=True)
 
         xt, grouped, x_codes, x_scales = {}, {}, {}, {}
         a_ps, v_ps, a_sb = {}, {}, {}
@@ -175,11 +182,16 @@ def tile_hydraencoderlayer_pa_t_kernel(tc, x, wk, wv, out):
             a_sb[n, j] = work.tile([P, DI], F32, name="a_sb")
             copy(out=a_sb[n, j][:], in_=a_ps[n, j][:])
 
-        def invert_norm(n):
+        def invert_norm(n, tiles=slice(0, PAIR)):
+            if n not in rnorm:
+                rnorm[n] = work.tile([P, PAIR], F32, name="rnorm")
             clamped = work.tile([P, PAIR], F32, name="clamped")
-            nc.gpsimd.tensor_scalar_max(out=clamped[:], in0=norm2[n][:], scalar1=EPS * EPS)
-            rnorm[n] = work.tile([P, PAIR], F32, name="rnorm")
-            nc.gpsimd.tensor_tensor(out=rnorm[n][:], in0=clamped[:], in1=minus_half[:], op=ALU.pow)
+            nc.gpsimd.tensor_scalar_max(
+                out=clamped[:, tiles], in0=norm2[n][:, tiles], scalar1=EPS * EPS
+            )
+            nc.gpsimd.tensor_tensor(
+                out=rnorm[n][:, tiles], in0=clamped[:, tiles], in1=minus_half[:, tiles], op=ALU.pow
+            )
 
         def product(n, j):
             if j == 0:
@@ -228,26 +240,37 @@ def tile_hydraencoderlayer_pa_t_kernel(tc, x, wk, wv, out):
                 transpose_x(n + 3, new_xt())
             if live(n - 2):
                 add_tokens(n - 2)
-            if live(n):
+            if live(n) and n < N_PAIRS - 2:
                 square_sum(n, 0)
-                if n < N_PAIRS - 1:
-                    copy_a(n, 0)
-                    square_sum(n, 1)
+                copy_a(n, 0)
+                square_sum(n, 1)
+                if n > 0:
                     copy_a(n, 1)
-                else:
-                    square_sum(n, 1)
-                    copy_a(n, 0)
                 invert_norm(n)
+            elif n == N_PAIRS - 2:
+                square_sum(n, 0)
+                invert_norm(n, slice(0, 1))
+                copy_a(n, 0)
+                square_sum(n, 1)
+                invert_norm(n, slice(1, 2))
+            elif n == N_PAIRS - 1:
+                for j in range(PAIR):
+                    square_sum(n, j)
+                    invert_norm(n, slice(j, j + 1))
+                copy_a(n - 1, 1)
+                copy_a(n, 0)
             if live(n + 1):
                 pass_a(n + 1, 1)
+            if n == 0:
+                copy_a(n, 1, copy=nc.vector.tensor_copy)
             if live(n - 1):
                 product(n - 1, 0)
             if live(n + 2):
                 quantise_x(n + 2)
-            if live(n - 1):
-                product(n - 1, 1)
             if n == N_PAIRS - 1:
                 copy_a(n, 1, copy=nc.vector.tensor_copy)
+            if live(n - 1):
+                product(n - 1, 1)
             if live(n):
                 pass_v(n, 1)
             if live(n - 2) and (n - 2) % PAIRS_PER_BATCH == PAIRS_PER_BATCH - 1:
@@ -255,11 +278,13 @@ def tile_hydraencoderlayer_pa_t_kernel(tc, x, wk, wv, out):
             if live(n + 3):
                 regroup_x(n + 3)
 
+        warm_up(6)
         interleave_weight("wk")
         quantise_weight("wk")
         banks = [new_xt(), new_xt(psum_v, "v_ps")]
         for j in range(PAIR):
             transpose_tile(banks[j], 0, j)
+        warm_up(2)
         for j in range(PAIR):
             regroup_tiles(0, slice(j, j + 1), banks[j], nc.scalar.copy)
             quantise_tiles(0, slice(j, j + 1))
@@ -268,8 +293,8 @@ def tile_hydraencoderlayer_pa_t_kernel(tc, x, wk, wv, out):
         interleave_weight("wv")
         transpose_x(1, new_xt(psum_v, "v_ps"))
         regroup_x(1)
-        quantise_weight("wv")
         quantise_x(1)
+        quantise_weight("wv")
         transpose_x(2, new_xt())
         regroup_x(2)
         for n in range(N_PAIRS + 2):

@@ -82,8 +82,8 @@ def tile_hydraencoderlayer_pa_t_kernel(tc, x, wk, wv, out):
             w_grouped[label] = consts.tile(
                 [P, DI, PACK], BF16, name="%s_grouped" % label, align_bytes=64
             )
-            w_codes[label] = consts.tile([P, DI], U32, name="%s_codes" % label, align_bytes=64)
-            w_scales[label] = consts.tile([P, DI], U8, name="%s_scales" % label, align_bytes=64)
+            w_codes[label] = consts.tile([P, DI], U32, name="%s_codes" % label, align_bytes=256)
+            w_scales[label] = consts.tile([P, DI], U8, name="%s_scales" % label, align_bytes=256)
 
         def quantise_weight(label):
             nc.vector.quantize_mx(
@@ -137,8 +137,8 @@ def tile_hydraencoderlayer_pa_t_kernel(tc, x, wk, wv, out):
 
         def quantise_tiles(n, tiles):
             if n not in x_codes:
-                x_codes[n] = operands.tile([P, PAIR * P], U32, name="x_codes", align_bytes=64)
-                x_scales[n] = operands.tile([P, PAIR * P], U8, name="x_scales", align_bytes=64)
+                x_codes[n] = operands.tile([P, PAIR * P], U32, name="x_codes", align_bytes=256)
+                x_scales[n] = operands.tile([P, PAIR * P], U8, name="x_scales", align_bytes=256)
             cols = slice(tiles.start * P, tiles.stop * P)
             nc.vector.quantize_mx(
                 out=x_codes[n][:, cols].bitcast(FP8X4),

@@ -72,8 +72,8 @@ def tile_hydraencoderlayer_pa_t_kernel(tc, x, wk, wv, out):
         nc.vector.memset(out_cols[:], 0.0)
         zeros = consts.tile([P, DI], BF16)
         nc.vector.memset(zeros[:], 0.0)
-        minus_half = consts.tile([P, PAIR], F32)
-        nc.vector.memset(minus_half[:], -0.5)
+        table_load = consts.tile([P, 1], F32)
+        nc.scalar.activation(out=table_load[:], in_=zeros[:, :1], func=ACT.Abs_reciprocal_sqrt, bias=1.0)
 
         w_grouped = {}
         w_codes = {}
@@ -105,8 +105,8 @@ def tile_hydraencoderlayer_pa_t_kernel(tc, x, wk, wv, out):
 
         xt, grouped, x_codes, x_scales = {}, {}, {}, {}
         a_ps, v_ps, a_sb = {}, {}, {}
-        norm2, rnorm = {}, {}
-        prod, token_sums = {}, {}
+        norm2, clamped, rnorm = {}, {}, {}
+        prod, pair_sum, token_sums = {}, {}, {}
 
         def transpose_tile(bank, n, j):
             x_words = x_chunks[n // PAIRS_PER_CHUNK][:].bitcast(F32)
@@ -182,16 +182,13 @@ def tile_hydraencoderlayer_pa_t_kernel(tc, x, wk, wv, out):
             a_sb[n, j] = work.tile([P, DI], F32, name="a_sb")
             copy(out=a_sb[n, j][:], in_=a_ps[n, j][:])
 
-        def invert_norm(n, tiles=slice(0, PAIR)):
-            if n not in rnorm:
-                rnorm[n] = work.tile([P, PAIR], F32, name="rnorm")
-            clamped = work.tile([P, PAIR], F32, name="clamped")
-            nc.gpsimd.tensor_scalar_max(
-                out=clamped[:, tiles], in0=norm2[n][:, tiles], scalar1=EPS * EPS
-            )
-            nc.gpsimd.tensor_tensor(
-                out=rnorm[n][:, tiles], in0=clamped[:, tiles], in1=minus_half[:, tiles], op=ALU.pow
-            )
+        def clamp_norm(n):
+            clamped[n] = work.tile([P, PAIR], F32, name="clamped")
+            nc.gpsimd.tensor_scalar_max(out=clamped[n][:], in0=norm2[n][:], scalar1=EPS * EPS)
+
+        def invert_norm(n):
+            rnorm[n] = work.tile([P, PAIR], F32, name="rnorm")
+            nc.scalar.activation(out=rnorm[n][:], in_=clamped[n][:], func=ACT.Abs_reciprocal_sqrt)
 
         def product(n, j):
             if j == 0:
@@ -205,19 +202,31 @@ def tile_hydraencoderlayer_pa_t_kernel(tc, x, wk, wv, out):
                 op1=ALU.mult,
             )
 
+        def add_pair(n):
+            if n % 4 != 1:
+                return
+            pair_sum[n] = work.tile([P, DI], F32, name="pair_sum")
+            nc.vector.tensor_tensor(
+                out=pair_sum[n][:], in0=prod[n][:, 0, :], in1=prod[n][:, 1, :], op=ALU.add
+            )
+
         def add_tokens(n):
             b, q = divmod(n, PAIRS_PER_BATCH)
             if q == 0:
                 token_sums[b] = psum_s.tile([P, E_BLOCKS, P], F32, name="token_sums")
-            for j in range(PAIR):
+            if n in pair_sum:
+                tiles = [pair_sum[n][:]]
+            else:
+                tiles = [prod[n][:, j, :] for j in range(PAIR)]
+            for k, tile in enumerate(tiles):
                 for i in range(E_BLOCKS):
                     nc.tensor.matmul(
                         out=token_sums[b][:, i, :],
-                        lhsT=prod[n][:, j, i * P : (i + 1) * P],
+                        lhsT=tile[:, i * P : (i + 1) * P],
                         rhs=ident[:],
                         is_transpose=True,
-                        start=(q == 0 and j == 0 and i == 0),
-                        stop=(q == PAIRS_PER_BATCH - 1 and j == PAIR - 1 and i == E_BLOCKS - 1),
+                        start=(q == 0 and k == 0 and i == 0),
+                        stop=(q == PAIRS_PER_BATCH - 1 and k == len(tiles) - 1 and i == E_BLOCKS - 1),
                     )
 
         def add_partitions(b):
@@ -240,24 +249,22 @@ def tile_hydraencoderlayer_pa_t_kernel(tc, x, wk, wv, out):
                 transpose_x(n + 3, new_xt())
             if live(n - 2):
                 add_tokens(n - 2)
-            if live(n) and n < N_PAIRS - 2:
+            if live(n) and n < N_PAIRS - 1:
                 square_sum(n, 0)
+                if live(n - 1):
+                    invert_norm(n - 1)
                 copy_a(n, 0)
                 square_sum(n, 1)
-                if n > 0:
+                clamp_norm(n)
+                if 0 < n < N_PAIRS - 2:
                     copy_a(n, 1)
-                invert_norm(n)
-            elif n == N_PAIRS - 2:
-                square_sum(n, 0)
-                invert_norm(n, slice(0, 1))
-                copy_a(n, 0)
-                square_sum(n, 1)
-                invert_norm(n, slice(1, 2))
             elif n == N_PAIRS - 1:
-                for j in range(PAIR):
-                    square_sum(n, j)
-                    invert_norm(n, slice(j, j + 1))
+                square_sum(n, 0)
+                invert_norm(n - 1)
+                square_sum(n, 1)
+                clamp_norm(n)
                 copy_a(n - 1, 1)
+                invert_norm(n)
                 copy_a(n, 0)
             if live(n + 1):
                 pass_a(n + 1, 1)
@@ -277,6 +284,8 @@ def tile_hydraencoderlayer_pa_t_kernel(tc, x, wk, wv, out):
                 add_partitions((n - 2) // PAIRS_PER_BATCH)
             if live(n + 3):
                 regroup_x(n + 3)
+            if live(n - 1):
+                add_pair(n - 1)
 
         warm_up(6)
         interleave_weight("wk")
@@ -288,10 +297,10 @@ def tile_hydraencoderlayer_pa_t_kernel(tc, x, wk, wv, out):
         for j in range(PAIR):
             regroup_tiles(0, slice(j, j + 1), banks[j], nc.scalar.copy)
             quantise_tiles(0, slice(j, j + 1))
-        for j in range(PAIR):
-            pass_a(0, j)
+        pass_a(0, 0)
         interleave_weight("wv")
         transpose_x(1, new_xt(psum_v, "v_ps"))
+        pass_a(0, 1)
         regroup_x(1)
         quantise_x(1)
         quantise_weight("wv")

from contextlib import ExitStack

import concourse.mybir as mybir
from concourse.masks import make_identity

F32 = mybir.dt.float32
BF16 = mybir.dt.bfloat16
U32 = mybir.dt.uint32
U8 = mybir.dt.uint8
FP8X4 = mybir.dt.float8_e4m3fn_x4
ACT = mybir.ActivationFunctionType
ALU = mybir.AluOpType

P = 128
PACK = 4
BATCH, TOKENS, D, DI = 4, 2048, 512, 512
EPS = 1e-12
WORDS = D // 2
HALVES = WORDS // P
PAIR = 2
CHUNK_TILES = 4
CHUNKS_PER_BATCH = TOKENS // (CHUNK_TILES * P)
PAIRS_PER_CHUNK = CHUNK_TILES // PAIR
PAIRS_PER_BATCH = CHUNKS_PER_BATCH * PAIRS_PER_CHUNK
N_PAIRS = BATCH * PAIRS_PER_BATCH
W_SPLIT = 320
E_BLOCKS = DI // P

FLOPS = 2 * 2 * BATCH * TOKENS * D * DI


def tile_hydraencoderlayer_pa_t_kernel(tc, x, wk, wv, out):
    nc = tc.nc
    with ExitStack() as ctx:
        ctx.enter_context(tc.manual_schedule())
        consts = ctx.enter_context(tc.tile_pool(name="consts", bufs=1))
        x_pool = ctx.enter_context(tc.tile_pool(name="x_pool", bufs=BATCH * CHUNKS_PER_BATCH))
        stage = ctx.enter_context(tc.tile_pool(name="stage", bufs=2))
        operands = ctx.enter_context(tc.tile_pool(name="operands", bufs=4))
        work = ctx.enter_context(tc.tile_pool(name="work", bufs=6))
        psum_t = ctx.enter_context(tc.psum_pool(name="psum_t", bufs=1))
        psum_a = ctx.enter_context(tc.psum_pool(name="psum_a", bufs=3))
        psum_v = ctx.enter_context(tc.psum_pool(name="psum_v", bufs=3))
        psum_s = ctx.enter_context(tc.psum_pool(name="psum_s", bufs=1))

        w_raw = {}

        def load_weight(label, w):
            w_raw[label] = consts.tile([P, PACK, DI], BF16, name="%s_raw" % label)
            nc.sync.dma_start(
                out=w_raw[label][:].rearrange("q (u e) c -> q u (e c)", u=HALVES),
                in_=w.rearrange("(u q e) c -> q u (e c)", u=HALVES, e=2),
            )
        load_weight("wk", wk)
        x_chunks = []
        for b in range(BATCH):
            chunks = x[b].rearrange("(p c t) k -> c p (t k)", c=CHUNKS_PER_BATCH, t=CHUNK_TILES)
            for c in range(CHUNKS_PER_BATCH):
                x_sb = x_pool.tile([P, CHUNK_TILES * D], BF16)
                x_chunks.append(x_sb)
                if b == 0 and c == 0:
                    pair_cols = PAIR * D
                    nc.sync.dma_start(out=x_sb[:, :pair_cols], in_=chunks[c][:, :pair_cols])
                    load_weight("wv", wv)
                    nc.sync.dma_start(out=x_sb[:, pair_cols:], in_=chunks[c][:, pair_cols:])
                else:
                    nc.sync.dma_start(out=x_sb[:], in_=chunks[c])

        ident = consts.tile([P, P], F32)
        make_identity(nc, ident[:])
        out_cols = consts.tile([P, P], F32)
        nc.vector.memset(out_cols[:], 0.0)
        zeros = consts.tile([P, DI], BF16)
        nc.vector.memset(zeros[:], 0.0)
        table_load = consts.tile([P, 1], F32)
        nc.scalar.activation(out=table_load[:], in_=zeros[:, :1], func=ACT.Abs_reciprocal_sqrt, bias=1.0)

        w_grouped = {}
        w_codes = {}
        w_scales = {}
        for label in ("wk", "wv"):
            w_grouped[label] = consts.tile(
                [P, DI, PACK], BF16, name="%s_grouped" % label, align_bytes=64
            )
            w_codes[label] = consts.tile([P, DI], U32, name="%s_codes" % label, align_bytes=256)
            w_scales[label] = consts.tile([P, DI], U8, name="%s_scales" % label, align_bytes=256)

        def quantise_weight(label):
            nc.vector.quantize_mx(
                out=w_codes[label][:].bitcast(FP8X4),
                scales=w_scales[label][:],
                in_=w_grouped[label][:].rearrange("q c t -> q (c t)"),
            )

        def interleave_weight(label):
            by_column = w_raw[label][:].rearrange("q t c -> q c t")
            grouped_w = w_grouped[label]
            nc.vector.tensor_copy(out=grouped_w[:, :W_SPLIT, :], in_=by_column[:, :W_SPLIT, :])
            nc.scalar.copy(out=grouped_w[:, W_SPLIT:, :], in_=by_column[:, W_SPLIT:, :])

        def warm_up(count):
            bank = psum_s.tile([P, DI], F32, name="token_sums")
            for k in range(count):
                nc.tensor.matmul(out=bank[:], lhsT=zeros[:, :P], rhs=zeros[:], start=True, stop=True)

        xt, grouped, x_codes, x_scales = {}, {}, {}, {}
        a_ps, v_ps, a_sb = {}, {}, {}
        norm2, clamped, rnorm = {}, {}, {}
        prod, pair_sum, token_sums = {}, {}, {}

        def transpose_tile(bank, n, j):
            x_words = x_chunks[n // PAIRS_PER_CHUNK][:].bitcast(F32)
            first_word = ((n % PAIRS_PER_CHUNK) * PAIR + j) * WORDS
            for u in range(HALVES):
                w0 = first_word + u * P
                nc.tensor.transpose(bank[:, j, u, :], x_words[:, w0 : w0 + P], ident[:])

        def new_xt(pool=psum_t, name="xt"):
            return pool.tile([P, PAIR, HALVES, P], F32, name=name)

        def transpose_x(n, bank):
            xt[n] = bank
            for j in range(PAIR):
                transpose_tile(bank, n, j)

        def regroup_tiles(n, tiles, bank, copy):
            if n not in grouped:
                grouped[n] = stage.tile([P, PAIR * P * PACK], BF16, name="grouped", align_bytes=64)
            words = grouped[n][:].bitcast(F32).rearrange("p (j r u) -> p j r u", j=PAIR, u=HALVES)
            copy(
                out=words[:, tiles, :, :],
                in_=bank[:].rearrange("p j u r -> p j r u")[:, tiles, :, :],
            )

        def regroup_x(n):
            regroup_tiles(n, slice(0, PAIR), xt[n], nc.vector.tensor_copy)

        def quantise_tiles(n, tiles):
            if n not in x_codes:
                x_codes[n] = operands.tile([P, PAIR * P], U32, name="x_codes", align_bytes=256)
                x_scales[n] = operands.tile([P, PAIR * P], U8, name="x_scales", align_bytes=256)
            cols = slice(tiles.start * P, tiles.stop * P)
            nc.vector.quantize_mx(
                out=x_codes[n][:, cols].bitcast(FP8X4),
                scales=x_scales[n][:, cols],
                in_=grouped[n][:, tiles.start * P * PACK : tiles.stop * P * PACK],
            )

        def quantise_x(n):
            quantise_tiles(n, slice(0, PAIR))

        def mx_pass(bank, n, j, label):
            cols = slice(j * P, (j + 1) * P)
            nc.tensor.matmul_mx(
                out=bank[:],
                lhsT=x_codes[n][:, cols].bitcast(FP8X4),
                lhsT_scale=x_scales[n][:, cols],
                rhs=w_codes[label][:].bitcast(FP8X4),
                rhs_scale=w_scales[label][:],
                start=True,
                stop=True,
            )

        def pass_a(n, j):
            a_ps[n, j] = psum_a.tile([P, DI], F32, name="a_ps")
            mx_pass(a_ps[n, j], n, j, "wk")

        def pass_v(n, j):
            v_ps[n, j] = psum_v.tile([P, DI], F32, name="v_ps")
            mx_pass(v_ps[n, j], n, j, "wv")

        def square_sum(n, j):
            if j == 0:
                norm2[n] = work.tile([P, PAIR], F32, name="norm2")
            squares = work.tile([P, DI], BF16, name="squares")
            nc.scalar.activation(
                out=squares[:], in_=a_ps[n, j][:], func=ACT.Square,
                accum_out=norm2[n][:, j : j + 1],
            )

        def copy_a(n, j, copy=nc.scalar.copy):
            a_sb[n, j] = work.tile([P, DI], F32, name="a_sb")
            copy(out=a_sb[n, j][:], in_=a_ps[n, j][:])

        def clamp_norm(n):
            clamped[n] = work.tile([P, PAIR], F32, name="clamped")
            nc.gpsimd.tensor_scalar_max(out=clamped[n][:], in0=norm2[n][:], scalar1=EPS * EPS)

        def invert_norm(n):
            rnorm[n] = work.tile([P, PAIR], F32, name="rnorm")
            nc.scalar.activation(out=rnorm[n][:], in_=clamped[n][:], func=ACT.Abs_reciprocal_sqrt)

        def product(n, j):
            if j == 0:
                prod[n] = work.tile([P, PAIR, DI], F32, name="prod")
            nc.vector.scalar_tensor_tensor(
                out=prod[n][:, j, :],
                in0=a_sb[n, j][:],
                scalar=rnorm[n][:, j : j + 1],
                in1=v_ps[n, j][:],
                op0=ALU.mult,
                op1=ALU.mult,
            )

        def add_pair(n):
            if n % 4 != 1:
                return
            pair_sum[n] = work.tile([P, DI], F32, name="pair_sum")
            nc.vector.tensor_tensor(
                out=pair_sum[n][:], in0=prod[n][:, 0, :], in1=prod[n][:, 1, :], op=ALU.add
            )

        def add_tokens(n):
            b, q = divmod(n, PAIRS_PER_BATCH)
            if q == 0:
                token_sums[b] = psum_s.tile([P, E_BLOCKS, P], F32, name="token_sums")
            if n in pair_sum:
                tiles = [pair_sum[n][:]]
            else:
                tiles = [prod[n][:, j, :] for j in range(PAIR)]
            for k, tile in enumerate(tiles):
                for i in range(E_BLOCKS):
                    nc.tensor.matmul(
                        out=token_sums[b][:, i, :],
                        lhsT=tile[:, i * P : (i + 1) * P],
                        rhs=ident[:],
                        is_transpose=True,
                        start=(q == 0 and k == 0 and i == 0),
                        stop=(q == PAIRS_PER_BATCH - 1 and k == len(tiles) - 1 and i == E_BLOCKS - 1),
                    )

        def add_partitions(b):
            nc.vector.tensor_reduce(
                out=out_cols[:, b * E_BLOCKS : (b + 1) * E_BLOCKS],
                in_=token_sums[b][:],
                axis=mybir.AxisListType.X,
                op=ALU.add,
            )

        def live(n):
            return 0 <= n < N_PAIRS

        def step(n):
            if live(n + 1):
                pass_a(n + 1, 0)
            if live(n):
                pass_v(n, 0)
            if live(n + 3):
                transpose_x(n + 3, new_xt())
            if live(n - 2):
                add_tokens(n - 2)
            if live(n) and n < N_PAIRS - 1:
                square_sum(n, 0)
                if live(n - 1):
                    invert_norm(n - 1)
                copy_a(n, 0)
                square_sum(n, 1)
                clamp_norm(n)
                if 0 < n < N_PAIRS - 2:
                    copy_a(n, 1)
            elif n == N_PAIRS - 1:
                square_sum(n, 0)
                invert_norm(n - 1)
                square_sum(n, 1)
                clamp_norm(n)
                copy_a(n - 1, 1)
                invert_norm(n)
                copy_a(n, 0)
            if live(n + 1):
                pass_a(n + 1, 1)
            if n == 0:
                copy_a(n, 1, copy=nc.vector.tensor_copy)
            if live(n - 1):
                product(n - 1, 0)
            if live(n + 2):
                quantise_x(n + 2)
            if n == N_PAIRS - 1:
                copy_a(n, 1, copy=nc.vector.tensor_copy)
            if live(n - 1):
                product(n - 1, 1)
            if live(n):
                pass_v(n, 1)
            if live(n - 2) and (n - 2) % PAIRS_PER_BATCH == PAIRS_PER_BATCH - 1:
                add_partitions((n - 2) // PAIRS_PER_BATCH)
            if live(n + 3):
                regroup_x(n + 3)
            if live(n - 1):
                add_pair(n - 1)

        warm_up(6)
        interleave_weight("wk")
        quantise_weight("wk")
        banks = [new_xt(), new_xt(psum_v, "v_ps")]
        for j in range(PAIR):
            transpose_tile(banks[j], 0, j)
        warm_up(2)
        for j in range(PAIR):
            regroup_tiles(0, slice(j, j + 1), banks[j], nc.scalar.copy)
            quantise_tiles(0, slice(j, j + 1))
        pass_a(0, 0)
        interleave_weight("wv")
        transpose_x(1, new_xt(psum_v, "v_ps"))
        pass_a(0, 1)
        regroup_x(1)
        quantise_x(1)
        quantise_weight("wv")
        transpose_x(2, new_xt())
        regroup_x(2)
        for n in range(N_PAIRS + 2):
            step(n)

        out_rows_ps = psum_t.tile([P, P], F32, name="xt")
        nc.tensor.transpose(out_rows_ps[:], out_cols[:], ident[:])
        out_rows = consts.tile([P, P], F32)
        nc.vector.tensor_copy(out=out_rows[:], in_=out_rows_ps[:])
        nc.sync.dma_start(
            out=out.rearrange("b o (i e) -> (b o i) e", i=E_BLOCKS),
            in_=out_rows[0 : BATCH * E_BLOCKS, :],
        )
